import numpy as np
import ml_dtypes


def mxq(x, axis, fmt="e4m3"):
    dtype, down = {"e4m3": (ml_dtypes.float8_e4m3fn, 7), "e5m2": (ml_dtypes.float8_e5m2, 14)}[fmt]
    v = np.moveaxis(np.asarray(x, np.float32).astype(ml_dtypes.bfloat16).astype(np.float64), axis, -1)
    blocks = v.reshape(v.shape[:-1] + (-1, 32))
    amax = np.abs(blocks).max(-1, keepdims=True)
    byte = np.maximum(np.where(amax > 0, np.frexp(amax)[1] - 1 + 127, 0) - down, 1)
    scale = np.exp2(byte - 127.0)
    codes = (blocks / scale).astype(np.float32).astype(dtype).astype(np.float64)
    return np.moveaxis((codes * scale).reshape(v.shape), -1, axis)


WIDE = False


def mx_kscale(k):
    if not WIDE:
        return np.ones(k)
    levels = np.array([10, -10, 5, -5, 0])
    if k % 512:
        return np.exp2(np.random.permutation(np.resize(levels, k // 32))).repeat(32)
    a = np.empty((k // 512, 16))
    for p in range(k // 512):
        a[p, :8] = np.random.permutation(np.resize(levels, 8))
        for g in range(8):
            far = levels[np.abs(levels - a[p, g]) >= 10]
            a[p, g + 8] = far[np.random.randint(len(far))]
    return np.exp2(a.ravel()).repeat(32)


BF16 = ml_dtypes.bfloat16


def bf(x):
    return np.asarray(x, np.float32).astype(BF16)


def f64(x):
    return np.asarray(x).astype(np.float64)


B, F0, FK, S1, S2, D = 8, 8, 128, 128, 1024, 16
M1 = F0 * FK
M2 = F0 * S1


def setup_inputs():
    u = mx_kscale(M2).reshape(F0, S1)[:, 0]
    t = mx_kscale(M1).reshape(F0, FK)[0]
    w1 = np.random.standard_normal((F0, FK, S1)) / np.sqrt(M1) / u[:, None, None] / t[None, :, None]
    w2 = np.random.standard_normal((F0, S1, S2)) / np.sqrt(M2) / u[:, None, None]
    return {"x": bf(np.random.standard_normal((B, F0, D)) * u[None, :, None]),
            "x1": bf(np.random.standard_normal((B, FK, D)) * t[None, :, None]),
            "w1": bf(w1.reshape(M1, S1)), "b1": bf(np.random.standard_normal(S1) * 0.2),
            "w2": bf(w2.reshape(M2, S2)), "b2": bf(np.random.standard_normal(S2) * 0.2)}


def reference(x, x1, w1, b1, w2, b2):
    x0 = f64(x).transpose(0, 2, 1)
    xk = f64(x1).transpose(0, 2, 1)
    z1 = (x0[:, :, :, None] * xk[:, :, None, :]).reshape(B, D, M1)
    o1 = (mxq(z1, 2, "e4m3") @ mxq(f64(w1), 0, "e4m3")) + f64(b1)
    z2 = (x0[:, :, :, None] * o1[:, :, None, :]).reshape(B, D, M2)
    o2 = (mxq(z2, 2, "e4m3") @ mxq(f64(w2), 0, "e4m3")) + f64(b2)
    return np.concatenate([o1.sum(axis=1), o2.sum(axis=1)], axis=1)

@@ -1,0 +1,254 @@
+from contextlib import ExitStack
+
+import concourse.mybir as mybir
+from concourse.masks import make_identity
+
+BF16 = mybir.dt.bfloat16
+F32 = mybir.dt.float32
+U32 = mybir.dt.uint32
+U8 = mybir.dt.uint8
+FP8X4 = mybir.dt.float8_e4m3fn_x4
+ADD = mybir.AluOpType.add
+MULT = mybir.AluOpType.mult
+X_AXIS = mybir.AxisListType.X
+
+P = 128
+PACK = 4
+B, F0, FK, S1, S2, D = 8, 8, 128, 128, 1024, 16
+TOK = B * D
+PASSES = F0 // PACK
+FIELDS = F0 // PASSES
+QUAD = FK // PACK
+HALF = 512
+HALVES = S2 // HALF
+BLOCKS = HALF // P
+RUN = 4
+VECTOR_COLS = 192
+OUT_BLOCKS = 1 + S2 // P
+
+FLOPS = 2 * TOK * F0 * FK * (S1 + S2)
+
+
+def regroup(copy, grouped, raw):
+    copy(
+        out=grouped.rearrange("p (q i) t -> p q t i", i=RUN),
+        in_=raw.rearrange("p t (q i) -> p q t i", i=RUN),
+    )
+
+
+def tile_cin_pa_s_kernel(tc, x, x1, w1, b1, w2, b2, out):
+    nc = tc.nc
+    with ExitStack() as ctx:
+        keep = ctx.enter_context(tc.tile_pool(name="keep", bufs=1))
+        psum = ctx.enter_context(tc.psum_pool(name="psum", bufs=1))
+        ctx.enter_context(tc.manual_schedule())
+
+
+        x_rows = keep.tile([P, D], BF16)
+        nc.vector.memset(x_rows[B * F0 : P, :], 0.0)
+        bias_rows = keep.tile([P, P], BF16)
+        nc.vector.memset(bias_rows[:], 0.0)
+        ident_bf = keep.tile([P, P], BF16)
+        make_identity(nc, ident_bf[:])
+        pooled = keep.tile([P, P], F32)
+        nc.gpsimd.memset(pooled[:], 0.0)
+        pooled_kb = pooled[:, 0 : B * OUT_BLOCKS].rearrange("p (b k) -> p k b", k=OUT_BLOCKS)
+
+        nc.sync.dma_start(out=x_rows[0 : B * F0, :], in_=x.rearrange("b i d -> (b i) d"))
+        x1_all = keep.tile([P, B, PACK, D], BF16)
+        for f in range(FIELDS):
+            nc.sync.dma_start(
+                out=x1_all[f * QUAD : (f + 1) * QUAD].rearrange("q b t d -> q b (t d)"),
+                in_=x1.rearrange("b (q t) d -> q b (t d)", t=PACK),
+            )
+        w1_raw = keep.tile([P, PASSES, PACK, S1], BF16)
+        nc.sync.dma_start(out=w1_raw[:], in_=w1.rearrange("(c p t) n -> p c t n", t=PACK, p=P))
+        nc.scalar.dma_start(out=bias_rows[0:1, :], in_=b1.rearrange("(o s) -> o s", o=1))
+        nc.scalar.dma_start(out=bias_rows[1:OUT_BLOCKS, :], in_=b2.rearrange("(k s) -> k s", s=P))
+        w2_rows = w2.rearrange("(c p t) n -> c p t n", t=PACK, p=P)
+        w2_raw = {}
+        for h in range(HALVES):
+            for c in range(PASSES):
+                w2_raw[c, h] = keep.tile([P, PACK, HALF], BF16, name="w2_raw_%d_%d" % (c, h))
+                nc.sync.dma_start(out=w2_raw[c, h][:], in_=w2_rows[c][:, :, h * HALF : (h + 1) * HALF])
+
+        w2_grouped = {}
+        w2_codes = {}
+        w2_scales = {}
+
+        def regroup_w2_scalar(c, h):
+            w2_grouped[c, h] = keep.tile([P, HALF, PACK], BF16, align_bytes=64, name="w2_grouped_%d_%d" % (c, h))
+            regroup(nc.scalar.copy, w2_grouped[c, h][:, VECTOR_COLS:HALF, :], w2_raw[c, h][:, :, VECTOR_COLS:HALF])
+
+        def regroup_w2_vector(c, h):
+            regroup(nc.vector.tensor_copy, w2_grouped[c, h][:, 0:VECTOR_COLS, :], w2_raw[c, h][:, :, 0:VECTOR_COLS])
+
+        def quantise_w2(c, h):
+            w2_codes[c, h] = keep.tile([P, HALF], U32, align_bytes=64, name="w2_codes_%d_%d" % (c, h))
+            w2_scales[c, h] = keep.tile([P, HALF], U8, align_bytes=64, name="w2_scales_%d_%d" % (c, h))
+            nc.vector.quantize_mx(
+                out=w2_codes[c, h][:].bitcast(FP8X4),
+                scales=w2_scales[c, h][:],
+                in_=w2_grouped[c, h][:].rearrange("p n t -> p (n t)"),
+            )
+
+        def quantise_both_passes(name, grouped):
+            codes = keep.tile([P, PASSES, P], U32, align_bytes=64, name=name + "_codes")
+            scales = keep.tile([P, PASSES, P], U8, align_bytes=64, name=name + "_scales")
+            nc.vector.quantize_mx(
+                out=codes[:].rearrange("p c n -> p (c n)").bitcast(FP8X4),
+                scales=scales[:].rearrange("p c n -> p (c n)"),
+                in_=grouped[:].rearrange("p c n t -> p (c n t)"),
+            )
+            return codes, scales
+
+        def multiply(acc, stationary, moving):
+            for c in range(PASSES):
+                nc.tensor.matmul_mx(
+                    out=acc,
+                    lhsT=stationary[c][0].bitcast(FP8X4),
+                    lhsT_scale=stationary[c][1],
+                    rhs=moving[c][0].bitcast(FP8X4),
+                    rhs_scale=moving[c][1],
+                    start=(c == 0),
+                    stop=(c == PASSES - 1),
+                )
+
+        acc2 = {}
+
+        def multiply_half(h):
+            acc2[h] = psum.tile([P, BLOCKS, TOK], F32, name="acc2_%d" % h)
+            for k in range(BLOCKS):
+                cols = slice(k * P, (k + 1) * P)
+                w2_block = [(w2_codes[c, h][:, cols], w2_scales[c, h][:, cols]) for c in range(PASSES)]
+                multiply(acc2[h][:, k, :], w2_block, z2_q)
+
+        def pool_half(h):
+            nc.vector.tensor_reduce(
+                out=pooled_kb[:, 1 + h * BLOCKS : 1 + (h + 1) * BLOCKS, :],
+                in_=acc2[h][:].rearrange("p k (b d) -> p k b d", d=D),
+                axis=X_AXIS,
+                op=ADD,
+            )
+
+        ident_bi = ident_bf[:, 0 : B * F0]
+        row_sample = keep.tile([P, B], F32)
+        nc.vector.tensor_reduce(out=row_sample[:], in_=ident_bi.rearrange("p (b i) -> p b i", i=F0), axis=X_AXIS, op=ADD)
+        row_field = keep.tile([P, F0], F32)
+        nc.vector.tensor_reduce(out=row_field[:], in_=ident_bi.rearrange("p (b i) -> p i b", i=F0), axis=X_AXIS, op=ADD)
+        field_cols = keep.tile([P, PASSES, P], BF16)
+        nc.vector.tensor_copy(
+            out=field_cols[:].rearrange("p c (f q) -> p (c f) q", q=QUAD),
+            in_=row_field[:].unsqueeze(2).to_broadcast([P, F0, QUAD]),
+        )
+        copies = P // OUT_BLOCKS + 1
+        bias_pick = keep.tile([P, copies, OUT_BLOCKS], BF16)
+        nc.vector.tensor_copy(
+            out=bias_pick[:], in_=ident_bf[:, 0:OUT_BLOCKS].unsqueeze(1).to_broadcast([P, copies, OUT_BLOCKS])
+        )
+        x_split = keep.tile([P, B, D], BF16)
+        nc.vector.tensor_tensor(
+            out=x_split[:],
+            in0=x_rows[:].unsqueeze(1).to_broadcast([P, B, D]),
+            in1=row_sample[:].unsqueeze(2).to_broadcast([P, B, D]),
+            op=MULT,
+        )
+        x_ps = psum.tile([P, PASSES, TOK], F32)
+        for c in range(PASSES):
+            nc.tensor.matmul(
+                out=x_ps[:, c, :],
+                lhsT=field_cols[:, c, :],
+                rhs=x_split[:].rearrange("p b d -> p (b d)"),
+                start=True,
+                stop=True,
+            )
+        bias_ps = psum.tile([P, 2, P], F32)
+        nc.tensor.matmul(
+            out=bias_ps[:, 0, :], lhsT=ident_bf[:, 0:1].to_broadcast([P, P]), rhs=bias_rows[:], start=True, stop=True
+        )
+        nc.tensor.matmul(
+            out=bias_ps[:, 1, :],
+            lhsT=bias_pick[:].rearrange("p r k -> p (r k)")[:, 0:P],
+            rhs=bias_rows[:],
+            start=True,
+            stop=True,
+        )
+
+        ident_f32 = keep.tile([P, P], F32)
+        nc.scalar.copy(out=ident_f32[:], in_=ident_bf[:])
+        x_sb = keep.tile([P, PASSES, TOK], F32)
+        nc.scalar.copy(out=x_sb[:], in_=x_ps[:])
+        bias_sb = keep.tile([P, 2, P], F32)
+        nc.scalar.copy(out=bias_sb[:], in_=bias_ps[:])
+        w1_grouped = keep.tile([P, PASSES, S1, PACK], BF16, align_bytes=64)
+        for c in range(PASSES):
+            regroup(nc.scalar.copy, w1_grouped[:, c], w1_raw[:, c])
+        for h in range(HALVES):
+            for c in range(PASSES):
+                regroup_w2_scalar(c, h)
+
+        z1 = keep.tile([P, PASSES, TOK, PACK], BF16, align_bytes=64)
+        for c in range(PASSES):
+            nc.vector.tensor_tensor(
+                out=z1[:, c].rearrange("p (b d) t -> p b d t", d=D),
+                in0=x1_all[:].rearrange("p b t d -> p b d t"),
+                in1=x_ps[:, c, :].rearrange("p (b d) -> p b d", d=D).unsqueeze(3).to_broadcast([P, B, D, PACK]),
+                op=MULT,
+            )
+        z1_codes, z1_scales = quantise_both_passes("z1", z1)
+        w1_codes, w1_scales = quantise_both_passes("w1", w1_grouped)
+        z1_q = [(z1_codes[:, c, :], z1_scales[:, c, :]) for c in range(PASSES)]
+        w1_q = [(w1_codes[:, c, :], w1_scales[:, c, :]) for c in range(PASSES)]
+        acc1 = psum.tile([TOK, S1], F32)
+        multiply(acc1[:], z1_q, w1_q)
+        acc1_s = psum.tile([S1, TOK], F32)
+        multiply(acc1_s[:], w1_q, z1_q)
+        regroup_w2_vector(0, 0)
+
+        o1_spread = keep.tile([TOK, PACK, FIELDS, QUAD], F32)
+
+        def spread(row):
+            by_t = row.rearrange("p (q t) -> p t q", t=PACK)
+            return by_t.unsqueeze(2).to_broadcast([TOK, PACK, FIELDS, QUAD])
+
+        nc.vector.tensor_tensor(out=o1_spread[:], in0=spread(acc1[:]), in1=spread(bias_sb[:, 0, :]), op=ADD)
+        o1_ps = psum.tile([P, PACK, TOK], F32)
+        for t in range(PACK):
+            nc.tensor.transpose(
+                out=o1_ps[:, t, :], in_=o1_spread[:, t].rearrange("p f q -> p (f q)"), identity=ident_f32[:]
+            )
+
+        quantise_w2(0, 0)
+        z2 = keep.tile([P, PASSES, TOK, PACK], BF16, align_bytes=64)
+        nc.vector.tensor_tensor(
+            out=z2[:],
+            in0=o1_ps[:].rearrange("p t n -> p n t").unsqueeze(1).to_broadcast([P, PASSES, TOK, PACK]),
+            in1=x_sb[:].unsqueeze(3).to_broadcast([P, PASSES, TOK, PACK]),
+            op=MULT,
+        )
+        regroup_w2_vector(1, 0)
+        z2_codes, z2_scales = quantise_both_passes("z2", z2)
+        z2_q = [(z2_codes[:, c, :], z2_scales[:, c, :]) for c in range(PASSES)]
+        quantise_w2(1, 0)
+        multiply_half(0)
+        regroup_w2_vector(0, 1)
+        regroup_w2_vector(1, 1)
+        quantise_w2(0, 1)
+        quantise_w2(1, 1)
+        multiply_half(1)
+
+        nc.vector.tensor_reduce(
+            out=pooled_kb[:, 0, :], in_=acc1_s[:].rearrange("p (b d) -> p b d", d=D), axis=X_AXIS, op=ADD
+        )
+        pool_half(0)
+        pool_half(1)
+
+        out_ps = psum.tile([P, P], F32)
+        nc.tensor.transpose(out=out_ps[:], in_=pooled[:], identity=ident_f32[:])
+        out_sb = keep.tile([P, P], F32)
+        nc.vector.scalar_tensor_tensor(
+            out=out_sb[:], in0=bias_sb[:, 1, :], scalar=float(D), in1=out_ps[:], op0=MULT, op1=ADD
+        )
+        out_rows = out.rearrange("b (k s) -> (b k) s", s=P)
+        nc.sync.dma_start(out=out_rows[0:64, :], in_=out_sb[0:64, :])
+        nc.sync.dma_start(out=out_rows[64 : B * OUT_BLOCKS, :], in_=out_sb[64 : B * OUT_BLOCKS, :])

@@ -23,7 +23,7 @@ HALF = 512
 HALVES = S2 // HALF
 BLOCKS = HALF // P
 RUN = 4
-VECTOR_COLS = 192
+VECTOR_COLS = 128
 OUT_BLOCKS = 1 + S2 // P
 
 FLOPS = 2 * TOK * F0 * FK * (S1 + S2)
@@ -63,8 +63,8 @@ def tile_cin_pa_s_kernel(tc, x, x1, w1, b1, w2, b2, out):
             )
         w1_raw = keep.tile([P, PASSES, PACK, S1], BF16)
         nc.sync.dma_start(out=w1_raw[:], in_=w1.rearrange("(c p t) n -> p c t n", t=PACK, p=P))
-        nc.scalar.dma_start(out=bias_rows[0:1, :], in_=b1.rearrange("(o s) -> o s", o=1))
-        nc.scalar.dma_start(out=bias_rows[1:OUT_BLOCKS, :], in_=b2.rearrange("(k s) -> k s", s=P))
+        nc.sync.dma_start(out=bias_rows[0:1, :], in_=b1.rearrange("(o s) -> o s", o=1))
+        nc.sync.dma_start(out=bias_rows[1:OUT_BLOCKS, :], in_=b2.rearrange("(k s) -> k s", s=P))
         w2_rows = w2.rearrange("(c p t) n -> c p t n", t=PACK, p=P)
         w2_raw = {}
         for h in range(HALVES):
@@ -176,17 +176,13 @@ def tile_cin_pa_s_kernel(tc, x, x1, w1, b1, w2, b2, out):
 
         ident_f32 = keep.tile([P, P], F32)
         nc.scalar.copy(out=ident_f32[:], in_=ident_bf[:])
-        x_sb = keep.tile([P, PASSES, TOK], F32)
-        nc.scalar.copy(out=x_sb[:], in_=x_ps[:])
-        bias_sb = keep.tile([P, 2, P], F32)
-        nc.scalar.copy(out=bias_sb[:], in_=bias_ps[:])
         w1_grouped = keep.tile([P, PASSES, S1, PACK], BF16, align_bytes=64)
         for c in range(PASSES):
             regroup(nc.scalar.copy, w1_grouped[:, c], w1_raw[:, c])
-        for h in range(HALVES):
-            for c in range(PASSES):
-                regroup_w2_scalar(c, h)
-
+        b1_by_t = keep.tile([P, PACK, QUAD], F32)
+        nc.scalar.copy(out=b1_by_t[:], in_=bias_ps[:, 0, :].rearrange("p (q t) -> p t q", t=PACK))
+        bias_sb = keep.tile([P, P], F32)
+        nc.scalar.copy(out=bias_sb[:], in_=bias_ps[:, 1, :])
         z1 = keep.tile([P, PASSES, TOK, PACK], BF16, align_bytes=64)
         for c in range(PASSES):
             nc.vector.tensor_tensor(
@@ -195,6 +191,11 @@ def tile_cin_pa_s_kernel(tc, x, x1, w1, b1, w2, b2, out):
                 in1=x_ps[:, c, :].rearrange("p (b d) -> p b d", d=D).unsqueeze(3).to_broadcast([P, B, D, PACK]),
                 op=MULT,
             )
+        x_sb = keep.tile([P, PASSES, TOK], F32)
+        nc.scalar.copy(out=x_sb[:], in_=x_ps[:])
+        for h in range(HALVES):
+            for c in range(PASSES):
+                regroup_w2_scalar(c, h)
         z1_codes, z1_scales = quantise_both_passes("z1", z1)
         w1_codes, w1_scales = quantise_both_passes("w1", w1_grouped)
         z1_q = [(z1_codes[:, c, :], z1_scales[:, c, :]) for c in range(PASSES)]
@@ -207,11 +208,12 @@ def tile_cin_pa_s_kernel(tc, x, x1, w1, b1, w2, b2, out):
 
         o1_spread = keep.tile([TOK, PACK, FIELDS, QUAD], F32)
 
-        def spread(row):
-            by_t = row.rearrange("p (q t) -> p t q", t=PACK)
-            return by_t.unsqueeze(2).to_broadcast([TOK, PACK, FIELDS, QUAD])
-
-        nc.vector.tensor_tensor(out=o1_spread[:], in0=spread(acc1[:]), in1=spread(bias_sb[:, 0, :]), op=ADD)
+        nc.vector.tensor_tensor(
+            out=o1_spread[:],
+            in0=acc1[:].rearrange("p (q t) -> p t q", t=PACK).unsqueeze(2).to_broadcast([TOK, PACK, FIELDS, QUAD]),
+            in1=b1_by_t[:].unsqueeze(2).to_broadcast([TOK, PACK, FIELDS, QUAD]),
+            op=ADD,
+        )
         o1_ps = psum.tile([P, PACK, TOK], F32)
         for t in range(PACK):
             nc.tensor.transpose(
@@ -247,7 +249,7 @@ def tile_cin_pa_s_kernel(tc, x, x1, w1, b1, w2, b2, out):
         nc.tensor.transpose(out=out_ps[:], in_=pooled[:], identity=ident_f32[:])
         out_sb = keep.tile([P, P], F32)
         nc.vector.scalar_tensor_tensor(
-            out=out_sb[:], in0=bias_sb[:, 1, :], scalar=float(D), in1=out_ps[:], op0=MULT, op1=ADD
+            out=out_sb[:], in0=bias_sb[:], scalar=float(D), in1=out_ps[:], op0=MULT, op1=ADD
         )
         out_rows = out.rearrange("b (k s) -> (b k) s", s=P)
         nc.sync.dma_start(out=out_rows[0:64, :], in_=out_sb[0:64, :])

@@ -23,7 +23,9 @@ HALF = 512
 HALVES = S2 // HALF
 BLOCKS = HALF // P
 RUN = 4
-VECTOR_COLS = 128
+VECTOR_COLS = 160
+STOP_1, STOP_2 = 288, 224
+PAIRS = PACK // 2
 OUT_BLOCKS = 1 + S2 // P
 
 FLOPS = 2 * TOK * F0 * FK * (S1 + S2)
@@ -64,7 +66,6 @@ def tile_cin_pa_s_kernel(tc, x, x1, w1, b1, w2, b2, out):
         w1_raw = keep.tile([P, PASSES, PACK, S1], BF16)
         nc.sync.dma_start(out=w1_raw[:], in_=w1.rearrange("(c p t) n -> p c t n", t=PACK, p=P))
         nc.sync.dma_start(out=bias_rows[0:1, :], in_=b1.rearrange("(o s) -> o s", o=1))
-        nc.sync.dma_start(out=bias_rows[1:OUT_BLOCKS, :], in_=b2.rearrange("(k s) -> k s", s=P))
         w2_rows = w2.rearrange("(c p t) n -> c p t n", t=PACK, p=P)
         w2_raw = {}
         for h in range(HALVES):
@@ -73,34 +74,24 @@ def tile_cin_pa_s_kernel(tc, x, x1, w1, b1, w2, b2, out):
                 nc.sync.dma_start(out=w2_raw[c, h][:], in_=w2_rows[c][:, :, h * HALF : (h + 1) * HALF])
 
         w2_grouped = {}
-        w2_codes = {}
-        w2_scales = {}
+        w2_q = {}
+        for h in range(HALVES):
+            for c in range(PASSES):
+                w2_grouped[c, h] = keep.tile([P, HALF, PACK], BF16, align_bytes=64, name="w2_grouped_%d_%d" % (c, h))
 
-        def regroup_w2_scalar(c, h):
-            w2_grouped[c, h] = keep.tile([P, HALF, PACK], BF16, align_bytes=64, name="w2_grouped_%d_%d" % (c, h))
-            regroup(nc.scalar.copy, w2_grouped[c, h][:, VECTOR_COLS:HALF, :], w2_raw[c, h][:, :, VECTOR_COLS:HALF])
+        def regroup_w2(copy, c, h, low, high):
+            regroup(copy, w2_grouped[c, h][:, low:high, :], w2_raw[c, h][:, :, low:high])
 
-        def regroup_w2_vector(c, h):
-            regroup(nc.vector.tensor_copy, w2_grouped[c, h][:, 0:VECTOR_COLS, :], w2_raw[c, h][:, :, 0:VECTOR_COLS])
+        def quantise(name, grouped, columns):
+            codes = keep.tile([P, columns], U32, align_bytes=64, name=name + "_codes")
+            scales = keep.tile([P, columns], U8, align_bytes=64, name=name + "_scales")
+            nc.vector.quantize_mx(out=codes[:].bitcast(FP8X4), scales=scales[:], in_=grouped)
+            return [(codes[:, n : n + P], scales[:, n : n + P]) for n in range(0, columns, P)], (codes, scales)
 
         def quantise_w2(c, h):
-            w2_codes[c, h] = keep.tile([P, HALF], U32, align_bytes=64, name="w2_codes_%d_%d" % (c, h))
-            w2_scales[c, h] = keep.tile([P, HALF], U8, align_bytes=64, name="w2_scales_%d_%d" % (c, h))
-            nc.vector.quantize_mx(
-                out=w2_codes[c, h][:].bitcast(FP8X4),
-                scales=w2_scales[c, h][:],
-                in_=w2_grouped[c, h][:].rearrange("p n t -> p (n t)"),
-            )
-
-        def quantise_both_passes(name, grouped):
-            codes = keep.tile([P, PASSES, P], U32, align_bytes=64, name=name + "_codes")
-            scales = keep.tile([P, PASSES, P], U8, align_bytes=64, name=name + "_scales")
-            nc.vector.quantize_mx(
-                out=codes[:].rearrange("p c n -> p (c n)").bitcast(FP8X4),
-                scales=scales[:].rearrange("p c n -> p (c n)"),
-                in_=grouped[:].rearrange("p c n t -> p (c n t)"),
-            )
-            return codes, scales
+            parts, whole = quantise("w2_%d_%d" % (c, h), w2_grouped[c, h][:].rearrange("p n t -> p (n t)"), HALF)
+            for k in range(BLOCKS):
+                w2_q[h * BLOCKS + k, c] = parts[k]
 
         def multiply(acc, stationary, moving):
             for c in range(PASSES):
@@ -114,19 +105,14 @@ def tile_cin_pa_s_kernel(tc, x, x1, w1, b1, w2, b2, out):
                     stop=(c == PASSES - 1),
                 )
 
-        acc2 = {}
+        def multiply_blocks(acc, first):
+            for k in range(acc.shape[1]):
+                multiply(acc[:, k, :], [w2_q[first + k, c] for c in range(PASSES)], z2_q)
 
-        def multiply_half(h):
-            acc2[h] = psum.tile([P, BLOCKS, TOK], F32, name="acc2_%d" % h)
-            for k in range(BLOCKS):
-                cols = slice(k * P, (k + 1) * P)
-                w2_block = [(w2_codes[c, h][:, cols], w2_scales[c, h][:, cols]) for c in range(PASSES)]
-                multiply(acc2[h][:, k, :], w2_block, z2_q)
-
-        def pool_half(h):
+        def pool_blocks(acc, row):
             nc.vector.tensor_reduce(
-                out=pooled_kb[:, 1 + h * BLOCKS : 1 + (h + 1) * BLOCKS, :],
-                in_=acc2[h][:].rearrange("p k (b d) -> p k b d", d=D),
+                out=pooled_kb[:, row : row + acc.shape[1], :],
+                in_=acc.rearrange("p k (b d) -> p k b d", d=D),
                 axis=X_AXIS,
                 op=ADD,
             )
@@ -153,7 +139,7 @@ def tile_cin_pa_s_kernel(tc, x, x1, w1, b1, w2, b2, out):
             in1=row_sample[:].unsqueeze(2).to_broadcast([P, B, D]),
             op=MULT,
         )
-        x_ps = psum.tile([P, PASSES, TOK], F32)
+        x_ps = psum.tile([P, PASSES + 1, TOK], F32)
         for c in range(PASSES):
             nc.tensor.matmul(
                 out=x_ps[:, c, :],
@@ -162,27 +148,29 @@ def tile_cin_pa_s_kernel(tc, x, x1, w1, b1, w2, b2, out):
                 start=True,
                 stop=True,
             )
-        bias_ps = psum.tile([P, 2, P], F32)
+        side_ps = psum.tile([P, 3, P], F32)
         nc.tensor.matmul(
-            out=bias_ps[:, 0, :], lhsT=ident_bf[:, 0:1].to_broadcast([P, P]), rhs=bias_rows[:], start=True, stop=True
-        )
-        nc.tensor.matmul(
-            out=bias_ps[:, 1, :],
-            lhsT=bias_pick[:].rearrange("p r k -> p (r k)")[:, 0:P],
-            rhs=bias_rows[:],
+            out=side_ps[:, 2, 0:F0],
+            lhsT=x_split[:].rearrange("p b d -> p (b d)"),
+            rhs=field_cols[:].rearrange("p c (f q) -> p (c f) q", q=QUAD)[:, :, 0],
             start=True,
             stop=True,
         )
+        nc.tensor.matmul(
+            out=side_ps[:, 0, :], lhsT=ident_bf[:, 0:1].to_broadcast([P, P]), rhs=bias_rows[:], start=True, stop=True
+        )
+        nc.sync.dma_start(out=bias_rows[1:OUT_BLOCKS, :], in_=b2.rearrange("(k s) -> k s", s=P))
 
         ident_f32 = keep.tile([P, P], F32)
         nc.scalar.copy(out=ident_f32[:], in_=ident_bf[:])
         w1_grouped = keep.tile([P, PASSES, S1, PACK], BF16, align_bytes=64)
         for c in range(PASSES):
             regroup(nc.scalar.copy, w1_grouped[:, c], w1_raw[:, c])
-        b1_by_t = keep.tile([P, PACK, QUAD], F32)
-        nc.scalar.copy(out=b1_by_t[:], in_=bias_ps[:, 0, :].rearrange("p (q t) -> p t q", t=PACK))
-        bias_sb = keep.tile([P, P], F32)
-        nc.scalar.copy(out=bias_sb[:], in_=bias_ps[:, 1, :])
+        b1_row = keep.tile([TOK, PAIRS, QUAD, 2], F32)
+        nc.scalar.copy(out=b1_row[:], in_=side_ps[:, 0, :].rearrange("p (q u e) -> p u q e", u=PAIRS, e=2))
+        x_token = keep.tile([TOK, F0], F32)
+        nc.scalar.copy(out=x_token[:], in_=side_ps[:, 2, 0:F0])
+
         z1 = keep.tile([P, PASSES, TOK, PACK], BF16, align_bytes=64)
         for c in range(PASSES):
             nc.vector.tensor_tensor(
@@ -191,65 +179,104 @@ def tile_cin_pa_s_kernel(tc, x, x1, w1, b1, w2, b2, out):
                 in1=x_ps[:, c, :].rearrange("p (b d) -> p b d", d=D).unsqueeze(3).to_broadcast([P, B, D, PACK]),
                 op=MULT,
             )
-        x_sb = keep.tile([P, PASSES, TOK], F32)
-        nc.scalar.copy(out=x_sb[:], in_=x_ps[:])
-        for h in range(HALVES):
-            for c in range(PASSES):
-                regroup_w2_scalar(c, h)
-        z1_codes, z1_scales = quantise_both_passes("z1", z1)
-        w1_codes, w1_scales = quantise_both_passes("w1", w1_grouped)
-        z1_q = [(z1_codes[:, c, :], z1_scales[:, c, :]) for c in range(PASSES)]
-        w1_q = [(w1_codes[:, c, :], w1_scales[:, c, :]) for c in range(PASSES)]
-        acc1 = psum.tile([TOK, S1], F32)
-        multiply(acc1[:], z1_q, w1_q)
-        acc1_s = psum.tile([S1, TOK], F32)
-        multiply(acc1_s[:], w1_q, z1_q)
-        regroup_w2_vector(0, 0)
+        z1_q, z1_whole = quantise("z1", z1[:].rearrange("p c n t -> p (c n t)"), PASSES * TOK)
+        w1_q, w1_whole = quantise("w1", w1_grouped[:].rearrange("p c n t -> p (c n t)"), PASSES * S1)
+        acc1 = psum.tile([P, 3, P], F32)
+        multiply(acc1[:, 0, :], z1_q, w1_q)
+        o1_by_s = x_ps[:, PASSES : PASSES + 1, :]
+        multiply(o1_by_s[:, 0, :], w1_q, z1_q)
+        out_ps = psum.tile([P, 2, P], F32)
 
-        o1_spread = keep.tile([TOK, PACK, FIELDS, QUAD], F32)
+        def keep_warm(times):
+            for i in range(times):
+                nc.tensor.matmul_mx(
+                    out=out_ps[:].rearrange("p c n -> p (c n)"),
+                    lhsT=w1_q[0][0].bitcast(FP8X4),
+                    lhsT_scale=w1_q[0][1],
+                    rhs=z1_whole[0][:].bitcast(FP8X4),
+                    rhs_scale=z1_whole[1][:],
+                    start=True,
+                    stop=True,
+                )
 
+        keep_warm(4)
+        regroup_w2(nc.scalar.copy, 0, 0, VECTOR_COLS, HALF)
+        regroup_w2(nc.vector.tensor_copy, 0, 0, 0, VECTOR_COLS)
+        regroup_w2(nc.vector.tensor_copy, 1, 0, 0, VECTOR_COLS)
+        regroup_w2(nc.scalar.copy, 1, 0, VECTOR_COLS, STOP_1)
+        o1 = keep.tile([TOK, PAIRS, QUAD, 2], F32)
         nc.vector.tensor_tensor(
-            out=o1_spread[:],
-            in0=acc1[:].rearrange("p (q t) -> p t q", t=PACK).unsqueeze(2).to_broadcast([TOK, PACK, FIELDS, QUAD]),
-            in1=b1_by_t[:].unsqueeze(2).to_broadcast([TOK, PACK, FIELDS, QUAD]),
+            out=o1[:],
+            in0=acc1[:, 0, :].rearrange("p (q u e) -> p u q e", u=PAIRS, e=2),
+            in1=b1_row[:],
             op=ADD,
         )
-        o1_ps = psum.tile([P, PACK, TOK], F32)
-        for t in range(PACK):
-            nc.tensor.transpose(
-                out=o1_ps[:, t, :], in_=o1_spread[:, t].rearrange("p f q -> p (f q)"), identity=ident_f32[:]
-            )
 
         quantise_w2(0, 0)
+
+        z2_token = keep.tile([TOK, PASSES, PAIRS, FIELDS, QUAD * 2], BF16, align_bytes=64)
+        o1_runs = o1[:].rearrange("p u q e -> p u (q e)")
+        for f in range(FIELDS):
+            nc.vector.tensor_scalar_mul(out=z2_token[:, 0, :, f, :], in0=o1_runs, scalar1=x_token[:, f : f + 1])
+        for f in range(FIELDS):
+            nc.scalar.activation(
+                out=z2_token[:, 1, :, f, :],
+                in_=o1_runs,
+                func=mybir.ActivationFunctionType.Copy,
+                scale=x_token[:, FIELDS + f : FIELDS + f + 1],
+            )
+        z2_ps = []
+        for c in range(PASSES):
+            turned = psum.tile([P, PAIRS, TOK], F32, name="z2_ps_%d" % c)
+            for u in range(PAIRS):
+                nc.tensor.transpose(
+                    out=turned[:, u, :],
+                    in_=z2_token[:, c, u].rearrange("p f r -> p (f r)").bitcast(F32),
+                    identity=ident_f32[:],
+                )
+            z2_ps.append(turned)
+        keep_warm(4)
+        regroup_w2(nc.scalar.copy, 1, 0, STOP_1, HALF)
+        regroup_w2(nc.scalar.copy, 0, 1, VECTOR_COLS, STOP_2)
+        regroup_w2(nc.vector.tensor_copy, 0, 1, 0, VECTOR_COLS)
         z2 = keep.tile([P, PASSES, TOK, PACK], BF16, align_bytes=64)
-        nc.vector.tensor_tensor(
-            out=z2[:],
-            in0=o1_ps[:].rearrange("p t n -> p n t").unsqueeze(1).to_broadcast([P, PASSES, TOK, PACK]),
-            in1=x_sb[:].unsqueeze(3).to_broadcast([P, PASSES, TOK, PACK]),
-            op=MULT,
+        for c, copy in ((0, nc.vector.tensor_copy), (1, nc.scalar.copy)):
+            copy(
+                out=z2[:, c].rearrange("p n t -> p (n t)").bitcast(F32).rearrange("p (n u) -> p n u", u=PAIRS),
+                in_=z2_ps[c][:].rearrange("p u n -> p n u"),
+            )
+
+        z2_q, z2_whole = quantise("z2", z2[:].rearrange("p c n t -> p (c n t)"), PASSES * TOK)
+        nc.tensor.matmul(
+            out=side_ps[:, 1, :],
+            lhsT=bias_pick[:].rearrange("p r k -> p (r k)")[:, 0:P],
+            rhs=bias_rows[:],
+            start=True,
+            stop=True,
         )
-        regroup_w2_vector(1, 0)
-        z2_codes, z2_scales = quantise_both_passes("z2", z2)
-        z2_q = [(z2_codes[:, c, :], z2_scales[:, c, :]) for c in range(PASSES)]
         quantise_w2(1, 0)
-        multiply_half(0)
-        regroup_w2_vector(0, 1)
-        regroup_w2_vector(1, 1)
+        acc2_low = psum.tile([P, 4, TOK], F32)
+        multiply_blocks(acc2_low[:], 0)
+        keep_warm(6)
+        regroup_w2(nc.scalar.copy, 0, 1, STOP_2, HALF)
+        regroup_w2(nc.scalar.copy, 1, 1, VECTOR_COLS, HALF)
+        regroup_w2(nc.vector.tensor_copy, 1, 1, 0, VECTOR_COLS)
         quantise_w2(0, 1)
+        pool_blocks(o1_by_s, 0)
+        pool_blocks(acc2_low[:], 1)
         quantise_w2(1, 1)
-        multiply_half(1)
+        acc2_high = psum.tile([P, 2, TOK], F32)
+        multiply_blocks(acc2_high[:], 4)
+        multiply_blocks(acc1[:, 1:3, :], 6)
+        pool_blocks(acc2_high[:], 5)
+        pool_blocks(acc1[:, 1:3, :], 7)
 
-        nc.vector.tensor_reduce(
-            out=pooled_kb[:, 0, :], in_=acc1_s[:].rearrange("p (b d) -> p b d", d=D), axis=X_AXIS, op=ADD
-        )
-        pool_half(0)
-        pool_half(1)
-
-        out_ps = psum.tile([P, P], F32)
-        nc.tensor.transpose(out=out_ps[:], in_=pooled[:], identity=ident_f32[:])
+        bias_sb = keep.tile([P, P], F32)
+        nc.scalar.copy(out=bias_sb[:], in_=side_ps[:, 1, :])
+        nc.tensor.transpose(out=out_ps[:, 0, :], in_=pooled[:], identity=ident_f32[:])
         out_sb = keep.tile([P, P], F32)
         nc.vector.scalar_tensor_tensor(
-            out=out_sb[:], in0=bias_sb[:], scalar=float(D), in1=out_ps[:], op0=MULT, op1=ADD
+            out=out_sb[:], in0=bias_sb[:], scalar=float(D), in1=out_ps[:, 0, :], op0=MULT, op1=ADD
         )
         out_rows = out.rearrange("b (k s) -> (b k) s", s=P)
         nc.sync.dma_start(out=out_rows[0:64, :], in_=out_sb[0:64, :])

@@ -23,8 +23,9 @@ HALF = 512
 HALVES = S2 // HALF
 BLOCKS = HALF // P
 RUN = 4
-VECTOR_COLS = 160
-STOP_1, STOP_2 = 288, 224
+VECTOR_COLS = 192
+STOP_1 = 320
+LAST_PARTS = ((0, 64, 256), (256, 128, 256))
 PAIRS = PACK // 2
 OUT_BLOCKS = 1 + S2 // P
 
@@ -82,16 +83,23 @@ def tile_cin_pa_s_kernel(tc, x, x1, w1, b1, w2, b2, out):
         def regroup_w2(copy, c, h, low, high):
             regroup(copy, w2_grouped[c, h][:, low:high, :], w2_raw[c, h][:, :, low:high])
 
+        def regroup_last(copy, part):
+            low, vector_cols, cols = LAST_PARTS[part]
+            middle = low + vector_cols
+            low, high = (low, middle) if copy == nc.vector.tensor_copy else (middle, low + cols)
+            regroup_w2(copy, 1, 1, low, high)
+
         def quantise(name, grouped, columns):
             codes = keep.tile([P, columns], U32, align_bytes=64, name=name + "_codes")
             scales = keep.tile([P, columns], U8, align_bytes=64, name=name + "_scales")
             nc.vector.quantize_mx(out=codes[:].bitcast(FP8X4), scales=scales[:], in_=grouped)
             return [(codes[:, n : n + P], scales[:, n : n + P]) for n in range(0, columns, P)], (codes, scales)
 
-        def quantise_w2(c, h):
-            parts, whole = quantise("w2_%d_%d" % (c, h), w2_grouped[c, h][:].rearrange("p n t -> p (n t)"), HALF)
-            for k in range(BLOCKS):
-                w2_q[h * BLOCKS + k, c] = parts[k]
+        def quantise_w2(c, h, low=0, high=HALF):
+            grouped = w2_grouped[c, h][:, low:high, :].rearrange("p n t -> p (n t)")
+            parts, whole = quantise("w2_%d_%d_%d" % (c, h, low), grouped, high - low)
+            for k, part in enumerate(parts):
+                w2_q[(h * HALF + low) // P + k, c] = part
 
         def multiply(acc, stationary, moving):
             for c in range(PASSES):
@@ -212,7 +220,7 @@ def tile_cin_pa_s_kernel(tc, x, x1, w1, b1, w2, b2, out):
             op=ADD,
         )
 
-        quantise_w2(0, 0)
+        pool_blocks(o1_by_s, 0)
 
         z2_token = keep.tile([TOK, PASSES, PAIRS, FIELDS, QUAD * 2], BF16, align_bytes=64)
         o1_runs = o1[:].rearrange("p u q e -> p u (q e)")
@@ -237,7 +245,7 @@ def tile_cin_pa_s_kernel(tc, x, x1, w1, b1, w2, b2, out):
             z2_ps.append(turned)
         keep_warm(4)
         regroup_w2(nc.scalar.copy, 1, 0, STOP_1, HALF)
-        regroup_w2(nc.scalar.copy, 0, 1, VECTOR_COLS, STOP_2)
+        quantise_w2(0, 0)
         regroup_w2(nc.vector.tensor_copy, 0, 1, 0, VECTOR_COLS)
         z2 = keep.tile([P, PASSES, TOK, PACK], BF16, align_bytes=64)
         for c, copy in ((0, nc.vector.tensor_copy), (1, nc.scalar.copy)):
@@ -245,6 +253,8 @@ def tile_cin_pa_s_kernel(tc, x, x1, w1, b1, w2, b2, out):
                 out=z2[:, c].rearrange("p n t -> p (n t)").bitcast(F32).rearrange("p (n u) -> p n u", u=PAIRS),
                 in_=z2_ps[c][:].rearrange("p u n -> p n u"),
             )
+
+        regroup_last(nc.vector.tensor_copy, 0)
 
         z2_q, z2_whole = quantise("z2", z2[:].rearrange("p c n t -> p (c n t)"), PASSES * TOK)
         nc.tensor.matmul(
@@ -258,15 +268,16 @@ def tile_cin_pa_s_kernel(tc, x, x1, w1, b1, w2, b2, out):
         acc2_low = psum.tile([P, 4, TOK], F32)
         multiply_blocks(acc2_low[:], 0)
         keep_warm(6)
-        regroup_w2(nc.scalar.copy, 0, 1, STOP_2, HALF)
-        regroup_w2(nc.scalar.copy, 1, 1, VECTOR_COLS, HALF)
-        regroup_w2(nc.vector.tensor_copy, 1, 1, 0, VECTOR_COLS)
+        regroup_w2(nc.scalar.copy, 0, 1, VECTOR_COLS, HALF)
+        regroup_last(nc.scalar.copy, 0)
+        regroup_last(nc.scalar.copy, 1)
+        regroup_last(nc.vector.tensor_copy, 1)
         quantise_w2(0, 1)
-        pool_blocks(o1_by_s, 0)
         pool_blocks(acc2_low[:], 1)
-        quantise_w2(1, 1)
+        quantise_w2(1, 1, 0, 256)
         acc2_high = psum.tile([P, 2, TOK], F32)
         multiply_blocks(acc2_high[:], 4)
+        quantise_w2(1, 1, 256, 512)
         multiply_blocks(acc1[:, 1:3, :], 6)
         pool_blocks(acc2_high[:], 5)
         pool_blocks(acc1[:, 1:3, :], 7)

@@ -23,9 +23,9 @@ HALF = 512
 HALVES = S2 // HALF
 BLOCKS = HALF // P
 RUN = 4
-VECTOR_COLS = 192
-STOP_1 = 320
-LAST_PARTS = ((0, 64, 256), (256, 128, 256))
+VECTOR_COLS = 224
+STOP_1, STOP_2 = 352, 304
+LAST_PARTS = ((0, 96, 256), (256, 128, 256))
 PAIRS = PACK // 2
 OUT_BLOCKS = 1 + S2 // P
 
@@ -60,7 +60,7 @@ def tile_cin_pa_s_kernel(tc, x, x1, w1, b1, w2, b2, out):
         nc.sync.dma_start(out=x_rows[0 : B * F0, :], in_=x.rearrange("b i d -> (b i) d"))
         x1_all = keep.tile([P, B, PACK, D], BF16)
         for f in range(FIELDS):
-            nc.sync.dma_start(
+            (nc.sync, nc.scalar)[f // 2].dma_start(
                 out=x1_all[f * QUAD : (f + 1) * QUAD].rearrange("q b t d -> q b (t d)"),
                 in_=x1.rearrange("b (q t) d -> q b (t d)", t=PACK),
             )
@@ -172,8 +172,10 @@ def tile_cin_pa_s_kernel(tc, x, x1, w1, b1, w2, b2, out):
         ident_f32 = keep.tile([P, P], F32)
         nc.scalar.copy(out=ident_f32[:], in_=ident_bf[:])
         w1_grouped = keep.tile([P, PASSES, S1, PACK], BF16, align_bytes=64)
-        for c in range(PASSES):
-            regroup(nc.scalar.copy, w1_grouped[:, c], w1_raw[:, c])
+        regroup(nc.scalar.copy, w1_grouped[:, 0], w1_raw[:, 0])
+        nc.gpsimd.tensor_scalar(
+            out=w1_grouped[:, 1], in0=w1_raw[:, 1].rearrange("p t n -> p n t"), scalar1=1.0, scalar2=0.0, op0=MULT, op1=ADD
+        )
         b1_row = keep.tile([TOK, PAIRS, QUAD, 2], F32)
         nc.scalar.copy(out=b1_row[:], in_=side_ps[:, 0, :].rearrange("p (q u e) -> p u q e", u=PAIRS, e=2))
         x_token = keep.tile([TOK, F0], F32)
@@ -187,8 +189,8 @@ def tile_cin_pa_s_kernel(tc, x, x1, w1, b1, w2, b2, out):
                 in1=x_ps[:, c, :].rearrange("p (b d) -> p b d", d=D).unsqueeze(3).to_broadcast([P, B, D, PACK]),
                 op=MULT,
             )
-        z1_q, z1_whole = quantise("z1", z1[:].rearrange("p c n t -> p (c n t)"), PASSES * TOK)
         w1_q, w1_whole = quantise("w1", w1_grouped[:].rearrange("p c n t -> p (c n t)"), PASSES * S1)
+        z1_q, z1_whole = quantise("z1", z1[:].rearrange("p c n t -> p (c n t)"), PASSES * TOK)
         acc1 = psum.tile([P, 3, P], F32)
         multiply(acc1[:, 0, :], z1_q, w1_q)
         o1_by_s = x_ps[:, PASSES : PASSES + 1, :]
@@ -245,17 +247,19 @@ def tile_cin_pa_s_kernel(tc, x, x1, w1, b1, w2, b2, out):
             z2_ps.append(turned)
         keep_warm(4)
         regroup_w2(nc.scalar.copy, 1, 0, STOP_1, HALF)
+        regroup_w2(nc.scalar.copy, 0, 1, VECTOR_COLS, STOP_2)
         quantise_w2(0, 0)
         regroup_w2(nc.vector.tensor_copy, 0, 1, 0, VECTOR_COLS)
         z2 = keep.tile([P, PASSES, TOK, PACK], BF16, align_bytes=64)
-        for c, copy in ((0, nc.vector.tensor_copy), (1, nc.scalar.copy)):
-            copy(
+        for c in range(PASSES):
+            nc.scalar.copy(
                 out=z2[:, c].rearrange("p n t -> p (n t)").bitcast(F32).rearrange("p (n u) -> p n u", u=PAIRS),
                 in_=z2_ps[c][:].rearrange("p u n -> p n u"),
             )
 
         regroup_last(nc.vector.tensor_copy, 0)
 
+        quantise_w2(1, 0)
         z2_q, z2_whole = quantise("z2", z2[:].rearrange("p c n t -> p (c n t)"), PASSES * TOK)
         nc.tensor.matmul(
             out=side_ps[:, 1, :],
@@ -264,11 +268,10 @@ def tile_cin_pa_s_kernel(tc, x, x1, w1, b1, w2, b2, out):
             start=True,
             stop=True,
         )
-        quantise_w2(1, 0)
         acc2_low = psum.tile([P, 4, TOK], F32)
         multiply_blocks(acc2_low[:], 0)
         keep_warm(6)
-        regroup_w2(nc.scalar.copy, 0, 1, VECTOR_COLS, HALF)
+        regroup_w2(nc.scalar.copy, 0, 1, STOP_2, HALF)
         regroup_last(nc.scalar.copy, 0)
         regroup_last(nc.scalar.copy, 1)
         regroup_last(nc.vector.tensor_copy, 1)

@@ -270,7 +270,6 @@ def tile_cin_pa_s_kernel(tc, x, x1, w1, b1, w2, b2, out):
         )
         acc2_low = psum.tile([P, 4, TOK], F32)
         multiply_blocks(acc2_low[:], 0)
-        keep_warm(6)
         regroup_w2(nc.scalar.copy, 0, 1, STOP_2, HALF)
         regroup_last(nc.scalar.copy, 0)
         regroup_last(nc.scalar.copy, 1)

from contextlib import ExitStack

import concourse.mybir as mybir
from concourse.masks import make_identity

BF16 = mybir.dt.bfloat16
F32 = mybir.dt.float32
U32 = mybir.dt.uint32
U8 = mybir.dt.uint8
FP8X4 = mybir.dt.float8_e4m3fn_x4
ADD = mybir.AluOpType.add
MULT = mybir.AluOpType.mult
X_AXIS = mybir.AxisListType.X

P = 128
PACK = 4
B, F0, FK, S1, S2, D = 8, 8, 128, 128, 1024, 16
TOK = B * D
PASSES = F0 // PACK
FIELDS = F0 // PASSES
QUAD = FK // PACK
HALF = 512
HALVES = S2 // HALF
BLOCKS = HALF // P
RUN = 4
VECTOR_COLS = 224
STOP_1, STOP_2 = 352, 304
LAST_PARTS = ((0, 96, 256), (256, 128, 256))
PAIRS = PACK // 2
OUT_BLOCKS = 1 + S2 // P

FLOPS = 2 * TOK * F0 * FK * (S1 + S2)


def regroup(copy, grouped, raw):
    copy(
        out=grouped.rearrange("p (q i) t -> p q t i", i=RUN),
        in_=raw.rearrange("p t (q i) -> p q t i", i=RUN),
    )


def tile_cin_pa_s_kernel(tc, x, x1, w1, b1, w2, b2, out):
    nc = tc.nc
    with ExitStack() as ctx:
        keep = ctx.enter_context(tc.tile_pool(name="keep", bufs=1))
        psum = ctx.enter_context(tc.psum_pool(name="psum", bufs=1))
        ctx.enter_context(tc.manual_schedule())


        x_rows = keep.tile([P, D], BF16)
        nc.vector.memset(x_rows[B * F0 : P, :], 0.0)
        bias_rows = keep.tile([P, P], BF16)
        nc.vector.memset(bias_rows[:], 0.0)
        ident_bf = keep.tile([P, P], BF16)
        make_identity(nc, ident_bf[:])
        pooled = keep.tile([P, P], F32)
        nc.gpsimd.memset(pooled[:], 0.0)
        pooled_kb = pooled[:, 0 : B * OUT_BLOCKS].rearrange("p (b k) -> p k b", k=OUT_BLOCKS)

        nc.sync.dma_start(out=x_rows[0 : B * F0, :], in_=x.rearrange("b i d -> (b i) d"))
        x1_all = keep.tile([P, B, PACK, D], BF16)
        for f in range(FIELDS):
            (nc.sync, nc.scalar)[f // 2].dma_start(
                out=x1_all[f * QUAD : (f + 1) * QUAD].rearrange("q b t d -> q b (t d)"),
                in_=x1.rearrange("b (q t) d -> q b (t d)", t=PACK),
            )
        w1_raw = keep.tile([P, PASSES, PACK, S1], BF16)
        nc.sync.dma_start(out=w1_raw[:], in_=w1.rearrange("(c p t) n -> p c t n", t=PACK, p=P))
        nc.sync.dma_start(out=bias_rows[0:1, :], in_=b1.rearrange("(o s) -> o s", o=1))
        w2_rows = w2.rearrange("(c p t) n -> c p t n", t=PACK, p=P)
        w2_raw = {}
        for h in range(HALVES):
            for c in range(PASSES):
                w2_raw[c, h] = keep.tile([P, PACK, HALF], BF16, name="w2_raw_%d_%d" % (c, h))
                nc.sync.dma_start(out=w2_raw[c, h][:], in_=w2_rows[c][:, :, h * HALF : (h + 1) * HALF])

        w2_grouped = {}
        w2_q = {}
        for h in range(HALVES):
            for c in range(PASSES):
                w2_grouped[c, h] = keep.tile([P, HALF, PACK], BF16, align_bytes=64, name="w2_grouped_%d_%d" % (c, h))

        def regroup_w2(copy, c, h, low, high):
            regroup(copy, w2_grouped[c, h][:, low:high, :], w2_raw[c, h][:, :, low:high])

        def regroup_last(copy, part):
            low, vector_cols, cols = LAST_PARTS[part]
            middle = low + vector_cols
            low, high = (low, middle) if copy == nc.vector.tensor_copy else (middle, low + cols)
            regroup_w2(copy, 1, 1, low, high)

        def quantise(name, grouped, columns):
            codes = keep.tile([P, columns], U32, align_bytes=64, name=name + "_codes")
            scales = keep.tile([P, columns], U8, align_bytes=64, name=name + "_scales")
            nc.vector.quantize_mx(out=codes[:].bitcast(FP8X4), scales=scales[:], in_=grouped)
            return [(codes[:, n : n + P], scales[:, n : n + P]) for n in range(0, columns, P)], (codes, scales)

        def quantise_w2(c, h, low=0, high=HALF):
            grouped = w2_grouped[c, h][:, low:high, :].rearrange("p n t -> p (n t)")
            parts, whole = quantise("w2_%d_%d_%d" % (c, h, low), grouped, high - low)
            for k, part in enumerate(parts):
                w2_q[(h * HALF + low) // P + k, c] = part

        def multiply(acc, stationary, moving):
            for c in range(PASSES):
                nc.tensor.matmul_mx(
                    out=acc,
                    lhsT=stationary[c][0].bitcast(FP8X4),
                    lhsT_scale=stationary[c][1],
                    rhs=moving[c][0].bitcast(FP8X4),
                    rhs_scale=moving[c][1],
                    start=(c == 0),
                    stop=(c == PASSES - 1),
                )

        def multiply_blocks(acc, first):
            for k in range(acc.shape[1]):
                multiply(acc[:, k, :], [w2_q[first + k, c] for c in range(PASSES)], z2_q)

        def pool_blocks(acc, row):
            nc.vector.tensor_reduce(
                out=pooled_kb[:, row : row + acc.shape[1], :],
                in_=acc.rearrange("p k (b d) -> p k b d", d=D),
                axis=X_AXIS,
                op=ADD,
            )

        ident_bi = ident_bf[:, 0 : B * F0]
        row_sample = keep.tile([P, B], F32)
        nc.vector.tensor_reduce(out=row_sample[:], in_=ident_bi.rearrange("p (b i) -> p b i", i=F0), axis=X_AXIS, op=ADD)
        row_field = keep.tile([P, F0], F32)
        nc.vector.tensor_reduce(out=row_field[:], in_=ident_bi.rearrange("p (b i) -> p i b", i=F0), axis=X_AXIS, op=ADD)
        field_cols = keep.tile([P, PASSES, P], BF16)
        nc.vector.tensor_copy(
            out=field_cols[:].rearrange("p c (f q) -> p (c f) q", q=QUAD),
            in_=row_field[:].unsqueeze(2).to_broadcast([P, F0, QUAD]),
        )
        copies = P // OUT_BLOCKS + 1
        bias_pick = keep.tile([P, copies, OUT_BLOCKS], BF16)
        nc.vector.tensor_copy(
            out=bias_pick[:], in_=ident_bf[:, 0:OUT_BLOCKS].unsqueeze(1).to_broadcast([P, copies, OUT_BLOCKS])
        )
        x_split = keep.tile([P, B, D], BF16)
        nc.vector.tensor_tensor(
            out=x_split[:],
            in0=x_rows[:].unsqueeze(1).to_broadcast([P, B, D]),
            in1=row_sample[:].unsqueeze(2).to_broadcast([P, B, D]),
            op=MULT,
        )
        x_ps = psum.tile([P, PASSES + 1, TOK], F32)
        for c in range(PASSES):
            nc.tensor.matmul(
                out=x_ps[:, c, :],
                lhsT=field_cols[:, c, :],
                rhs=x_split[:].rearrange("p b d -> p (b d)"),
                start=True,
                stop=True,
            )
        side_ps = psum.tile([P, 3, P], F32)
        nc.tensor.matmul(
            out=side_ps[:, 2, 0:F0],
            lhsT=x_split[:].rearrange("p b d -> p (b d)"),
            rhs=field_cols[:].rearrange("p c (f q) -> p (c f) q", q=QUAD)[:, :, 0],
            start=True,
            stop=True,
        )
        nc.tensor.matmul(
            out=side_ps[:, 0, :], lhsT=ident_bf[:, 0:1].to_broadcast([P, P]), rhs=bias_rows[:], start=True, stop=True
        )
        nc.sync.dma_start(out=bias_rows[1:OUT_BLOCKS, :], in_=b2.rearrange("(k s) -> k s", s=P))

        ident_f32 = keep.tile([P, P], F32)
        nc.scalar.copy(out=ident_f32[:], in_=ident_bf[:])
        w1_grouped = keep.tile([P, PASSES, S1, PACK], BF16, align_bytes=64)
        regroup(nc.scalar.copy, w1_grouped[:, 0], w1_raw[:, 0])
        nc.gpsimd.tensor_scalar(
            out=w1_grouped[:, 1], in0=w1_raw[:, 1].rearrange("p t n -> p n t"), scalar1=1.0, scalar2=0.0, op0=MULT, op1=ADD
        )
        b1_row = keep.tile([TOK, PAIRS, QUAD, 2], F32)
        nc.scalar.copy(out=b1_row[:], in_=side_ps[:, 0, :].rearrange("p (q u e) -> p u q e", u=PAIRS, e=2))
        x_token = keep.tile([TOK, F0], F32)
        nc.scalar.copy(out=x_token[:], in_=side_ps[:, 2, 0:F0])

        z1 = keep.tile([P, PASSES, TOK, PACK], BF16, align_bytes=64)
        for c in range(PASSES):
            nc.vector.tensor_tensor(
                out=z1[:, c].rearrange("p (b d) t -> p b d t", d=D),
                in0=x1_all[:].rearrange("p b t d -> p b d t"),
                in1=x_ps[:, c, :].rearrange("p (b d) -> p b d", d=D).unsqueeze(3).to_broadcast([P, B, D, PACK]),
                op=MULT,
            )
        w1_q, w1_whole = quantise("w1", w1_grouped[:].rearrange("p c n t -> p (c n t)"), PASSES * S1)
        z1_q, z1_whole = quantise("z1", z1[:].rearrange("p c n t -> p (c n t)"), PASSES * TOK)
        acc1 = psum.tile([P, 3, P], F32)
        multiply(acc1[:, 0, :], z1_q, w1_q)
        o1_by_s = x_ps[:, PASSES : PASSES + 1, :]
        multiply(o1_by_s[:, 0, :], w1_q, z1_q)
        out_ps = psum.tile([P, 2, P], F32)

        def keep_warm(times):
            for i in range(times):
                nc.tensor.matmul_mx(
                    out=out_ps[:].rearrange("p c n -> p (c n)"),
                    lhsT=w1_q[0][0].bitcast(FP8X4),
                    lhsT_scale=w1_q[0][1],
                    rhs=z1_whole[0][:].bitcast(FP8X4),
                    rhs_scale=z1_whole[1][:],
                    start=True,
                    stop=True,
                )

        keep_warm(4)
        regroup_w2(nc.scalar.copy, 0, 0, VECTOR_COLS, HALF)
        regroup_w2(nc.vector.tensor_copy, 0, 0, 0, VECTOR_COLS)
        regroup_w2(nc.vector.tensor_copy, 1, 0, 0, VECTOR_COLS)
        regroup_w2(nc.scalar.copy, 1, 0, VECTOR_COLS, STOP_1)
        o1 = keep.tile([TOK, PAIRS, QUAD, 2], F32)
        nc.vector.tensor_tensor(
            out=o1[:],
            in0=acc1[:, 0, :].rearrange("p (q u e) -> p u q e", u=PAIRS, e=2),
            in1=b1_row[:],
            op=ADD,
        )

        pool_blocks(o1_by_s, 0)

        z2_token = keep.tile([TOK, PASSES, PAIRS, FIELDS, QUAD * 2], BF16, align_bytes=64)
        o1_runs = o1[:].rearrange("p u q e -> p u (q e)")
        for f in range(FIELDS):
            nc.vector.tensor_scalar_mul(out=z2_token[:, 0, :, f, :], in0=o1_runs, scalar1=x_token[:, f : f + 1])
        for f in range(FIELDS):
            nc.scalar.activation(
                out=z2_token[:, 1, :, f, :],
                in_=o1_runs,
                func=mybir.ActivationFunctionType.Copy,
                scale=x_token[:, FIELDS + f : FIELDS + f + 1],
            )
        z2_ps = []
        for c in range(PASSES):
            turned = psum.tile([P, PAIRS, TOK], F32, name="z2_ps_%d" % c)
            for u in range(PAIRS):
                nc.tensor.transpose(
                    out=turned[:, u, :],
                    in_=z2_token[:, c, u].rearrange("p f r -> p (f r)").bitcast(F32),
                    identity=ident_f32[:],
                )
            z2_ps.append(turned)
        keep_warm(4)
        regroup_w2(nc.scalar.copy, 1, 0, STOP_1, HALF)
        regroup_w2(nc.scalar.copy, 0, 1, VECTOR_COLS, STOP_2)
        quantise_w2(0, 0)
        regroup_w2(nc.vector.tensor_copy, 0, 1, 0, VECTOR_COLS)
        z2 = keep.tile([P, PASSES, TOK, PACK], BF16, align_bytes=64)
        for c in range(PASSES):
            nc.scalar.copy(
                out=z2[:, c].rearrange("p n t -> p (n t)").bitcast(F32).rearrange("p (n u) -> p n u", u=PAIRS),
                in_=z2_ps[c][:].rearrange("p u n -> p n u"),
            )

        regroup_last(nc.vector.tensor_copy, 0)

        quantise_w2(1, 0)
        z2_q, z2_whole = quantise("z2", z2[:].rearrange("p c n t -> p (c n t)"), PASSES * TOK)
        nc.tensor.matmul(
            out=side_ps[:, 1, :],
            lhsT=bias_pick[:].rearrange("p r k -> p (r k)")[:, 0:P],
            rhs=bias_rows[:],
            start=True,
            stop=True,
        )
        acc2_low = psum.tile([P, 4, TOK], F32)
        multiply_blocks(acc2_low[:], 0)
        regroup_w2(nc.scalar.copy, 0, 1, STOP_2, HALF)
        regroup_last(nc.scalar.copy, 0)
        regroup_last(nc.scalar.copy, 1)
        regroup_last(nc.vector.tensor_copy, 1)
        quantise_w2(0, 1)
        pool_blocks(acc2_low[:], 1)
        quantise_w2(1, 1, 0, 256)
        acc2_high = psum.tile([P, 2, TOK], F32)
        multiply_blocks(acc2_high[:], 4)
        quantise_w2(1, 1, 256, 512)
        multiply_blocks(acc1[:, 1:3, :], 6)
        pool_blocks(acc2_high[:], 5)
        pool_blocks(acc1[:, 1:3, :], 7)

        bias_sb = keep.tile([P, P], F32)
        nc.scalar.copy(out=bias_sb[:], in_=side_ps[:, 1, :])
        nc.tensor.transpose(out=out_ps[:, 0, :], in_=pooled[:], identity=ident_f32[:])
        out_sb = keep.tile([P, P], F32)
        nc.vector.scalar_tensor_tensor(
            out=out_sb[:], in0=bias_sb[:], scalar=float(D), in1=out_ps[:, 0, :], op0=MULT, op1=ADD
        )
        out_rows = out.rearrange("b (k s) -> (b k) s", s=P)
        nc.sync.dma_start(out=out_rows[0:64, :], in_=out_sb[0:64, :])
        nc.sync.dma_start(out=out_rows[64 : B * OUT_BLOCKS, :], in_=out_sb[64 : B * OUT_BLOCKS, :])
